import numpy as np
import ml_dtypes


def mxq(x, axis, fmt="e4m3"):
    dtype, down = {"e4m3": (ml_dtypes.float8_e4m3fn, 7), "e5m2": (ml_dtypes.float8_e5m2, 14)}[fmt]
    v = np.moveaxis(np.asarray(x, np.float32).astype(ml_dtypes.bfloat16).astype(np.float64), axis, -1)
    blocks = v.reshape(v.shape[:-1] + (-1, 32))
    amax = np.abs(blocks).max(-1, keepdims=True)
    byte = np.maximum(np.where(amax > 0, np.frexp(amax)[1] - 1 + 127, 0) - down, 1)
    scale = np.exp2(byte - 127.0)
    codes = (blocks / scale).astype(np.float32).astype(dtype).astype(np.float64)
    return np.moveaxis((codes * scale).reshape(v.shape), -1, axis)


WIDE = False


def mx_kscale(k):
    if not WIDE:
        return np.ones(k)
    levels = np.array([10, -10, 5, -5, 0])
    a = np.random.permutation(np.resize(levels, k // 512 * 4)).reshape(k // 512, 4)
    idx = np.arange(k)
    return np.exp2(a[idx // 512, idx % 128 // 32])


BF16 = ml_dtypes.bfloat16


def bf(x):
    return np.asarray(x, np.float32).astype(BF16)


def f64(x):
    return np.asarray(x).astype(np.float64)


B, S, DIM, HID, R, NT = 8, 512, 512, 1024, 128, 3
SCALING = 4.0


def lora_out(xa, bw, tw):
    return (xa @ bw) * SCALING * tw[..., None]


def setup_inputs():
    s = mx_kscale(HID)
    return {"h": bf(np.random.standard_normal((B, S, HID)) * 0.7 * s),
            "w2": bf(np.random.standard_normal((HID, DIM)) / np.sqrt(HID) / s[:, None]),
            "ha_down": bf(np.random.standard_normal((B, S, R)) * 0.7),
            "b_down": bf(np.random.standard_normal((R, DIM)) * 0.2 / np.sqrt(R)),
            "tw_down": bf(np.random.uniform(size=(B, S)))}


def reference(h, w2, ha_down, b_down, tw_down):
    base = mxq(f64(h), 2, "e4m3") @ mxq(f64(w2), 0, "e4m3")
    return base + lora_out(f64(ha_down), f64(b_down), f64(tw_down))

@@ -1,0 +1,146 @@
+from contextlib import ExitStack
+
+import concourse.mybir as mybir
+from concourse.masks import make_identity
+
+BF16 = mybir.dt.bfloat16
+F32 = mybir.dt.float32
+U32 = mybir.dt.uint32
+U8 = mybir.dt.uint8
+FP8X4 = mybir.dt.float8_e4m3fn_x4
+COPY = mybir.ActivationFunctionType.Copy
+ADD = mybir.AluOpType.add
+
+P = 128
+TOKENS = 8 * 512
+HID = 1024
+DIM = 512
+RANK = 128
+SCALING = 4.0
+
+PACK = 4
+K_PASS = P * PACK
+PASSES = HID // K_PASS
+HALVES = 2
+
+TILES = TOKENS // P
+ROUND = 4
+ROUNDS = TILES // ROUND
+HA_CHUNK = 8
+HA_CHUNKS = TILES // HA_CHUNK
+
+FLOPS = 2 * TOKENS * HID * DIM + 2 * TOKENS * RANK * DIM
+
+
+def tile_feedforward_pb_t_kernel(tc, h, w2, ha_down, b_down, tw_down, out):
+    nc = tc.nc
+    h_view = h.flatten_outer_dims().rearrange("(p t) k -> p t k", t=TILES)
+    ha_view = ha_down.flatten_outer_dims().rearrange("(p t) r -> p t r", t=TILES)
+    tw_view = tw_down.rearrange("b (q t) -> (b q) t", t=TILES)
+    out_view = out.flatten_outer_dims().rearrange("(p t) n -> p t n", t=TILES)
+
+    with ExitStack() as ctx:
+        keep = ctx.enter_context(tc.tile_pool(name="keep", bufs=1))
+        stage = ctx.enter_context(tc.tile_pool(name="stage", bufs=2 * ROUND))
+        psum = ctx.enter_context(tc.psum_pool(name="psum", bufs=4))
+
+        ha_sb = [keep.tile([P, HA_CHUNK, RANK], BF16, name="ha%d" % c) for c in range(HA_CHUNKS)]
+        b_sb = keep.tile([P, DIM], BF16, name="b_sb")
+        tw_sb = keep.tile([P, TILES], BF16, name="tw_sb")
+        w_raw = keep.tile([P, PASSES, PACK, DIM], BF16, name="w_raw")
+        h_sb = [keep.tile([P, ROUND, HID], BF16, name="h%d" % r) for r in range(ROUNDS)]
+
+        nc.sync.dma_start(out=ha_sb[0][:], in_=ha_view[:, 0:HA_CHUNK, :])
+        nc.sync.dma_start(out=b_sb[:], in_=b_down)
+        nc.sync.dma_start(out=tw_sb[:], in_=tw_view)
+        for c in range(1, HA_CHUNKS):
+            nc.sync.dma_start(out=ha_sb[c][:], in_=ha_view[:, c * HA_CHUNK : (c + 1) * HA_CHUNK, :])
+        for g in range(PASSES):
+            nc.sync.dma_start(
+                out=w_raw[:, g].rearrange("q (u e) n -> q u e n", u=HALVES),
+                in_=w2[g * K_PASS : (g + 1) * K_PASS, :].rearrange("(u q e) n -> q u e n", u=HALVES, q=P),
+            )
+        for r in range(ROUNDS):
+            nc.sync.dma_start(out=h_sb[r][:], in_=h_view[:, r * ROUND : (r + 1) * ROUND, :])
+
+        ident_bf16 = keep.tile([P, P], BF16, name="ident_bf16")
+        make_identity(nc, ident_bf16[:])
+        ident_f32 = keep.tile([P, P], F32, name="ident_f32")
+        make_identity(nc, ident_f32[:])
+        gain = keep.tile([P, TILES], F32, name="gain")
+        nc.vector.tensor_scalar_mul(out=gain[:], in0=tw_sb[:], scalar1=SCALING)
+
+        out_sb = [keep.tile([P, ROUND, DIM], F32, name="out%d" % r) for r in range(ROUNDS)]
+        for c in range(HA_CHUNKS):
+            haT_ps = psum.tile([P, HA_CHUNK, P], BF16, tag="transposed")
+            for j in range(HA_CHUNK):
+                nc.tensor.transpose(haT_ps[:, j, :], ha_sb[c][:, j, :], ident_bf16[:])
+            haT_sb = keep.tile([P, HA_CHUNK, P], BF16, name="haT%d" % c)
+            nc.vector.tensor_copy(out=haT_sb[:], in_=haT_ps[:])
+            for j in range(HA_CHUNK):
+                t = c * HA_CHUNK + j
+                lora_ps = psum.tile([P, DIM], F32, tag="product")
+                nc.tensor.matmul(lora_ps[:], lhsT=haT_sb[:, j, :], rhs=b_sb[:], start=True, stop=True)
+                scaled = out_sb[t // ROUND][:, t % ROUND, :]
+                if t % 3 == 2:
+                    nc.vector.tensor_scalar_mul(out=scaled, in0=lora_ps[:], scalar1=gain[:, t : t + 1])
+                else:
+                    nc.scalar.activation(out=scaled, in_=lora_ps[:], func=COPY, scale=gain[:, t : t + 1])
+
+        w_grouped = keep.tile([P, PASSES, DIM, PACK], BF16, name="w_grouped", align_bytes=64)
+        w_codes = keep.tile([P, PASSES, DIM], U32, name="w_codes", align_bytes=64)
+        w_scales = keep.tile([P, PASSES, DIM], U8, name="w_scales", align_bytes=64)
+        for g in range(PASSES):
+            nc.vector.tensor_copy(out=w_grouped[:, g], in_=w_raw[:, g].rearrange("q t n -> q n t"))
+        for g in range(PASSES):
+            nc.vector.quantize_mx(
+                out=w_codes[:, g, :].bitcast(FP8X4),
+                scales=w_scales[:, g, :],
+                in_=w_grouped[:, g].rearrange("q n t -> q (n t)"),
+            )
+
+        def transpose_and_quantise(r):
+            h_words = h_sb[r][:].bitcast(F32)
+            quantised = []
+            for a in range(ROUND):
+                hT_ps = psum.tile([P, PASSES * HALVES, P], F32, tag="transposed")
+                for s in range(PASSES * HALVES):
+                    nc.tensor.transpose(hT_ps[:, s, :], h_words[:, a, s * P : (s + 1) * P], ident_f32[:])
+                h_grouped = stage.tile([P, PASSES, P, PACK], BF16, tag="h_grouped", align_bytes=64)
+                nc.scalar.copy(
+                    out=h_grouped[:].bitcast(F32),
+                    in_=hT_ps[:].rearrange("q (g u) m -> q g m u", u=HALVES),
+                )
+                h_codes = stage.tile([P, PASSES, P], U32, tag="h_codes", align_bytes=64)
+                h_scales = stage.tile([P, PASSES, P], U8, tag="h_scales", align_bytes=64)
+                nc.vector.quantize_mx(
+                    out=h_codes[:].rearrange("q g m -> q (g m)").bitcast(FP8X4),
+                    scales=h_scales[:].rearrange("q g m -> q (g m)"),
+                    in_=h_grouped[:].rearrange("q g m t -> q (g m t)"),
+                )
+                quantised.append((h_codes, h_scales))
+            return quantised
+
+        def project_and_store(r, quantised):
+            for a in range(ROUND):
+                h_codes, h_scales = quantised[a]
+                base_ps = psum.tile([P, DIM], F32, tag="product")
+                for g in range(PASSES):
+                    nc.tensor.matmul_mx(
+                        out=base_ps[:],
+                        lhsT=h_codes[:, g, :].bitcast(FP8X4),
+                        lhsT_scale=h_scales[:, g, :],
+                        rhs=w_codes[:, g, :].bitcast(FP8X4),
+                        rhs_scale=w_scales[:, g, :],
+                        start=(g == 0),
+                        stop=(g == PASSES - 1),
+                    )
+                nc.vector.tensor_tensor(out=out_sb[r][:, a, :], in0=base_ps[:], in1=out_sb[r][:, a, :], op=ADD)
+            nc.sync.dma_start(out=out_view[:, r * ROUND : (r + 1) * ROUND, :], in_=out_sb[r][:])
+
+        ahead = transpose_and_quantise(0)
+        for r in range(ROUNDS):
+            current = ahead
+            if r + 1 < ROUNDS:
+                ahead = transpose_and_quantise(r + 1)
+            project_and_store(r, current)

@@ -26,8 +26,11 @@ HALVES = 2
 TILES = TOKENS // P
 ROUND = 4
 ROUNDS = TILES // ROUND
+STORE = 2
 HA_CHUNK = 8
 HA_CHUNKS = TILES // HA_CHUNK
+
+assert HA_CHUNKS == 2 * PASSES
 
 FLOPS = 2 * TOKENS * HID * DIM + 2 * TOKENS * RANK * DIM
 
@@ -44,15 +47,17 @@ def tile_feedforward_pb_t_kernel(tc, h, w2, ha_down, b_down, tw_down, out):
         stage = ctx.enter_context(tc.tile_pool(name="stage", bufs=2 * ROUND))
         psum = ctx.enter_context(tc.psum_pool(name="psum", bufs=4))
 
+        ctx.enter_context(tc.manual_schedule())
+
         ha_sb = [keep.tile([P, HA_CHUNK, RANK], BF16, name="ha%d" % c) for c in range(HA_CHUNKS)]
         b_sb = keep.tile([P, DIM], BF16, name="b_sb")
         tw_sb = keep.tile([P, TILES], BF16, name="tw_sb")
         w_raw = keep.tile([P, PASSES, PACK, DIM], BF16, name="w_raw")
         h_sb = [keep.tile([P, ROUND, HID], BF16, name="h%d" % r) for r in range(ROUNDS)]
 
+        nc.sync.dma_start(out=tw_sb[:], in_=tw_view)
         nc.sync.dma_start(out=ha_sb[0][:], in_=ha_view[:, 0:HA_CHUNK, :])
         nc.sync.dma_start(out=b_sb[:], in_=b_down)
-        nc.sync.dma_start(out=tw_sb[:], in_=tw_view)
         for c in range(1, HA_CHUNKS):
             nc.sync.dma_start(out=ha_sb[c][:], in_=ha_view[:, c * HA_CHUNK : (c + 1) * HA_CHUNK, :])
         for g in range(PASSES):
@@ -70,38 +75,50 @@ def tile_feedforward_pb_t_kernel(tc, h, w2, ha_down, b_down, tw_down, out):
         gain = keep.tile([P, TILES], F32, name="gain")
         nc.vector.tensor_scalar_mul(out=gain[:], in0=tw_sb[:], scalar1=SCALING)
 
-        out_sb = [keep.tile([P, ROUND, DIM], F32, name="out%d" % r) for r in range(ROUNDS)]
-        for c in range(HA_CHUNKS):
-            haT_ps = psum.tile([P, HA_CHUNK, P], BF16, tag="transposed")
-            for j in range(HA_CHUNK):
-                nc.tensor.transpose(haT_ps[:, j, :], ha_sb[c][:, j, :], ident_bf16[:])
-            haT_sb = keep.tile([P, HA_CHUNK, P], BF16, name="haT%d" % c)
-            nc.vector.tensor_copy(out=haT_sb[:], in_=haT_ps[:])
-            for j in range(HA_CHUNK):
-                t = c * HA_CHUNK + j
-                lora_ps = psum.tile([P, DIM], F32, tag="product")
-                nc.tensor.matmul(lora_ps[:], lhsT=haT_sb[:, j, :], rhs=b_sb[:], start=True, stop=True)
-                scaled = out_sb[t // ROUND][:, t % ROUND, :]
-                if t % 3 == 2:
-                    nc.vector.tensor_scalar_mul(out=scaled, in0=lora_ps[:], scalar1=gain[:, t : t + 1])
-                else:
-                    nc.scalar.activation(out=scaled, in_=lora_ps[:], func=COPY, scale=gain[:, t : t + 1])
-
         w_grouped = keep.tile([P, PASSES, DIM, PACK], BF16, name="w_grouped", align_bytes=64)
         w_codes = keep.tile([P, PASSES, DIM], U32, name="w_codes", align_bytes=64)
         w_scales = keep.tile([P, PASSES, DIM], U8, name="w_scales", align_bytes=64)
-        for g in range(PASSES):
+
+        def regroup_w2(g):
             nc.vector.tensor_copy(out=w_grouped[:, g], in_=w_raw[:, g].rearrange("q t n -> q n t"))
-        for g in range(PASSES):
+
+        def quantise_w2(g):
             nc.vector.quantize_mx(
                 out=w_codes[:, g, :].bitcast(FP8X4),
                 scales=w_scales[:, g, :],
                 in_=w_grouped[:, g].rearrange("q n t -> q (n t)"),
             )
 
-        def transpose_and_quantise(r):
+        out_sb = [keep.tile([P, ROUND, DIM], F32, name="out%d" % r) for r in range(ROUNDS)]
+        haT_sb = [keep.tile([P, HA_CHUNK, P], BF16, name="haT%d" % c) for c in range(HA_CHUNKS)]
+
+        def transpose_ha(c):
+            haT_ps = psum.tile([P, HA_CHUNK, P], BF16, tag="transposed")
+            for j in range(HA_CHUNK):
+                nc.tensor.transpose(haT_ps[:, j, :], ha_sb[c][:, j, :], ident_bf16[:])
+            nc.vector.tensor_copy(out=haT_sb[c][:], in_=haT_ps[:])
+
+        transpose_ha(0)
+        for c in range(HA_CHUNKS):
+            if c + 1 < HA_CHUNKS:
+                transpose_ha(c + 1)
+            for j in range(HA_CHUNK):
+                t = c * HA_CHUNK + j
+                lora_ps = psum.tile([P, DIM], F32, tag="product")
+                nc.tensor.matmul(lora_ps[:], lhsT=haT_sb[c][:, j, :], rhs=b_sb[:], start=True, stop=True)
+                scaled = out_sb[t // ROUND][:, t % ROUND, :]
+                if t % 3 == 2:
+                    nc.vector.tensor_scalar_mul(out=scaled, in0=lora_ps[:], scalar1=gain[:, t : t + 1])
+                else:
+                    nc.scalar.activation(out=scaled, in_=lora_ps[:], func=COPY, scale=gain[:, t : t + 1])
+            if c < PASSES:
+                regroup_w2(c)
+            else:
+                quantise_w2(c - PASSES)
+
+        def transpose_h(r):
             h_words = h_sb[r][:].bitcast(F32)
-            quantised = []
+            grouped = []
             for a in range(ROUND):
                 hT_ps = psum.tile([P, PASSES * HALVES, P], F32, tag="transposed")
                 for s in range(PASSES * HALVES):
@@ -111,36 +128,45 @@ def tile_feedforward_pb_t_kernel(tc, h, w2, ha_down, b_down, tw_down, out):
                     out=h_grouped[:].bitcast(F32),
                     in_=hT_ps[:].rearrange("q (g u) m -> q g m u", u=HALVES),
                 )
-                h_codes = stage.tile([P, PASSES, P], U32, tag="h_codes", align_bytes=64)
-                h_scales = stage.tile([P, PASSES, P], U8, tag="h_scales", align_bytes=64)
-                nc.vector.quantize_mx(
-                    out=h_codes[:].rearrange("q g m -> q (g m)").bitcast(FP8X4),
-                    scales=h_scales[:].rearrange("q g m -> q (g m)"),
-                    in_=h_grouped[:].rearrange("q g m t -> q (g m t)"),
+                grouped.append(h_grouped)
+            return grouped
+
+        def quantise_h(h_grouped):
+            h_codes = stage.tile([P, PASSES, P], U32, tag="h_codes", align_bytes=64)
+            h_scales = stage.tile([P, PASSES, P], U8, tag="h_scales", align_bytes=64)
+            nc.vector.quantize_mx(
+                out=h_codes[:].rearrange("q g m -> q (g m)").bitcast(FP8X4),
+                scales=h_scales[:].rearrange("q g m -> q (g m)"),
+                in_=h_grouped[:].rearrange("q g m t -> q (g m t)"),
+            )
+            return h_codes, h_scales
+
+        def project(r, a, h_codes, h_scales):
+            base_ps = psum.tile([P, DIM], F32, tag="product")
+            for g in range(PASSES):
+                nc.tensor.matmul_mx(
+                    out=base_ps[:],
+                    lhsT=h_codes[:, g, :].bitcast(FP8X4),
+                    lhsT_scale=h_scales[:, g, :],
+                    rhs=w_codes[:, g, :].bitcast(FP8X4),
+                    rhs_scale=w_scales[:, g, :],
+                    start=(g == 0),
+                    stop=(g == PASSES - 1),
                 )
-                quantised.append((h_codes, h_scales))
-            return quantised
+            return base_ps
 
-        def project_and_store(r, quantised):
-            for a in range(ROUND):
-                h_codes, h_scales = quantised[a]
-                base_ps = psum.tile([P, DIM], F32, tag="product")
-                for g in range(PASSES):
-                    nc.tensor.matmul_mx(
-                        out=base_ps[:],
-                        lhsT=h_codes[:, g, :].bitcast(FP8X4),
-                        lhsT_scale=h_scales[:, g, :],
-                        rhs=w_codes[:, g, :].bitcast(FP8X4),
-                        rhs_scale=w_scales[:, g, :],
-                        start=(g == 0),
-                        stop=(g == PASSES - 1),
-                    )
-                nc.vector.tensor_tensor(out=out_sb[r][:, a, :], in0=base_ps[:], in1=out_sb[r][:, a, :], op=ADD)
-            nc.sync.dma_start(out=out_view[:, r * ROUND : (r + 1) * ROUND, :], in_=out_sb[r][:])
-
-        ahead = transpose_and_quantise(0)
+        quantised = [quantise_h(h_grouped) for h_grouped in transpose_h(0)]
         for r in range(ROUNDS):
-            current = ahead
-            if r + 1 < ROUNDS:
-                ahead = transpose_and_quantise(r + 1)
-            project_and_store(r, current)
+            current = quantised
+            grouped = transpose_h(r + 1) if r + 1 < ROUNDS else []
+            quantised = []
+            for a in range(ROUND):
+                base_ps = project(r, a, current[a][0], current[a][1])
+                if grouped:
+                    quantised.append(quantise_h(grouped[a]))
+                nc.vector.tensor_tensor(out=out_sb[r][:, a, :], in0=base_ps[:], in1=out_sb[r][:, a, :], op=ADD)
+                if a % STORE == STORE - 1:
+                    first = r * ROUND + a + 1 - STORE
+                    nc.sync.dma_start(
+                        out=out_view[:, first : first + STORE, :], in_=out_sb[r][:, a + 1 - STORE : a + 1, :]
+                    )

@@ -8,7 +8,7 @@ F32 = mybir.dt.float32
 U32 = mybir.dt.uint32
 U8 = mybir.dt.uint8
 FP8X4 = mybir.dt.float8_e4m3fn_x4
-COPY = mybir.ActivationFunctionType.Copy
+MULT = mybir.AluOpType.mult
 ADD = mybir.AluOpType.add
 
 P = 128
@@ -26,7 +26,7 @@ HALVES = 2
 TILES = TOKENS // P
 ROUND = 4
 ROUNDS = TILES // ROUND
-STORE = 2
+STORE = 1
 HA_CHUNK = 8
 HA_CHUNKS = TILES // HA_CHUNK
 
@@ -106,11 +106,11 @@ def tile_feedforward_pb_t_kernel(tc, h, w2, ha_down, b_down, tw_down, out):
                 t = c * HA_CHUNK + j
                 lora_ps = psum.tile([P, DIM], F32, tag="product")
                 nc.tensor.matmul(lora_ps[:], lhsT=haT_sb[c][:, j, :], rhs=b_sb[:], start=True, stop=True)
-                scaled = out_sb[t // ROUND][:, t % ROUND, :]
+                lora_sb = out_sb[t // ROUND][:, t % ROUND, :]
                 if t % 3 == 2:
-                    nc.vector.tensor_scalar_mul(out=scaled, in0=lora_ps[:], scalar1=gain[:, t : t + 1])
+                    nc.vector.tensor_copy(out=lora_sb, in_=lora_ps[:])
                 else:
-                    nc.scalar.activation(out=scaled, in_=lora_ps[:], func=COPY, scale=gain[:, t : t + 1])
+                    nc.scalar.copy(out=lora_sb, in_=lora_ps[:])
             if c < PASSES:
                 regroup_w2(c)
             else:
@@ -164,7 +164,15 @@ def tile_feedforward_pb_t_kernel(tc, h, w2, ha_down, b_down, tw_down, out):
                 base_ps = project(r, a, current[a][0], current[a][1])
                 if grouped:
                     quantised.append(quantise_h(grouped[a]))
-                nc.vector.tensor_tensor(out=out_sb[r][:, a, :], in0=base_ps[:], in1=out_sb[r][:, a, :], op=ADD)
+                t = r * ROUND + a
+                nc.vector.scalar_tensor_tensor(
+                    out=out_sb[r][:, a, :],
+                    in0=out_sb[r][:, a, :],
+                    scalar=gain[:, t : t + 1],
+                    in1=base_ps[:],
+                    op0=MULT,
+                    op1=ADD,
+                )
                 if a % STORE == STORE - 1:
                     first = r * ROUND + a + 1 - STORE
                     nc.sync.dma_start(

@@ -24,13 +24,12 @@ PASSES = HID // K_PASS
 HALVES = 2
 
 TILES = TOKENS // P
-ROUND = 4
+ROUND = 2
 ROUNDS = TILES // ROUND
-STORE = 1
 HA_CHUNK = 8
 HA_CHUNKS = TILES // HA_CHUNK
-
-assert HA_CHUNKS == 2 * PASSES
+LEAD = HA_CHUNK // ROUND
+BANKS = 4
 
 FLOPS = 2 * TOKENS * HID * DIM + 2 * TOKENS * RANK * DIM
 
@@ -44,27 +43,29 @@ def tile_feedforward_pb_t_kernel(tc, h, w2, ha_down, b_down, tw_down, out):
 
     with ExitStack() as ctx:
         keep = ctx.enter_context(tc.tile_pool(name="keep", bufs=1))
-        stage = ctx.enter_context(tc.tile_pool(name="stage", bufs=2 * ROUND))
-        psum = ctx.enter_context(tc.psum_pool(name="psum", bufs=4))
-
+        stage = ctx.enter_context(tc.tile_pool(name="stage", bufs=3))
+        psum = ctx.enter_context(tc.psum_pool(name="psum", bufs=BANKS))
         ctx.enter_context(tc.manual_schedule())
 
+        tw_sb = keep.tile([P, TILES], BF16, name="tw_sb")
         ha_sb = [keep.tile([P, HA_CHUNK, RANK], BF16, name="ha%d" % c) for c in range(HA_CHUNKS)]
         b_sb = keep.tile([P, DIM], BF16, name="b_sb")
-        tw_sb = keep.tile([P, TILES], BF16, name="tw_sb")
         w_raw = keep.tile([P, PASSES, PACK, DIM], BF16, name="w_raw")
         h_sb = [keep.tile([P, ROUND, HID], BF16, name="h%d" % r) for r in range(ROUNDS)]
 
-        nc.sync.dma_start(out=tw_sb[:], in_=tw_view)
-        nc.sync.dma_start(out=ha_sb[0][:], in_=ha_view[:, 0:HA_CHUNK, :])
-        nc.sync.dma_start(out=b_sb[:], in_=b_down)
-        for c in range(1, HA_CHUNKS):
+        def load_ha(c):
             nc.sync.dma_start(out=ha_sb[c][:], in_=ha_view[:, c * HA_CHUNK : (c + 1) * HA_CHUNK, :])
+
+        nc.sync.dma_start(out=tw_sb[:], in_=tw_view)
+        load_ha(0)
+        nc.sync.dma_start(out=b_sb[:], in_=b_down)
         for g in range(PASSES):
             nc.sync.dma_start(
                 out=w_raw[:, g].rearrange("q (u e) n -> q u e n", u=HALVES),
                 in_=w2[g * K_PASS : (g + 1) * K_PASS, :].rearrange("(u q e) n -> q u e n", u=HALVES, q=P),
             )
+        for c in range(1, HA_CHUNKS):
+            load_ha(c)
         for r in range(ROUNDS):
             nc.sync.dma_start(out=h_sb[r][:], in_=h_view[:, r * ROUND : (r + 1) * ROUND, :])
 
@@ -75,22 +76,8 @@ def tile_feedforward_pb_t_kernel(tc, h, w2, ha_down, b_down, tw_down, out):
         gain = keep.tile([P, TILES], F32, name="gain")
         nc.vector.tensor_scalar_mul(out=gain[:], in0=tw_sb[:], scalar1=SCALING)
 
-        w_grouped = keep.tile([P, PASSES, DIM, PACK], BF16, name="w_grouped", align_bytes=64)
-        w_codes = keep.tile([P, PASSES, DIM], U32, name="w_codes", align_bytes=64)
-        w_scales = keep.tile([P, PASSES, DIM], U8, name="w_scales", align_bytes=64)
-
-        def regroup_w2(g):
-            nc.vector.tensor_copy(out=w_grouped[:, g], in_=w_raw[:, g].rearrange("q t n -> q n t"))
-
-        def quantise_w2(g):
-            nc.vector.quantize_mx(
-                out=w_codes[:, g, :].bitcast(FP8X4),
-                scales=w_scales[:, g, :],
-                in_=w_grouped[:, g].rearrange("q n t -> q (n t)"),
-            )
-
-        out_sb = [keep.tile([P, ROUND, DIM], F32, name="out%d" % r) for r in range(ROUNDS)]
         haT_sb = [keep.tile([P, HA_CHUNK, P], BF16, name="haT%d" % c) for c in range(HA_CHUNKS)]
+        out_sb = [keep.tile([P, ROUND, DIM], F32, name="out%d" % r) for r in range(ROUNDS)]
 
         def transpose_ha(c):
             haT_ps = psum.tile([P, HA_CHUNK, P], BF16, tag="transposed")
@@ -98,56 +85,59 @@ def tile_feedforward_pb_t_kernel(tc, h, w2, ha_down, b_down, tw_down, out):
                 nc.tensor.transpose(haT_ps[:, j, :], ha_sb[c][:, j, :], ident_bf16[:])
             nc.vector.tensor_copy(out=haT_sb[c][:], in_=haT_ps[:])
 
-        transpose_ha(0)
-        for c in range(HA_CHUNKS):
-            if c + 1 < HA_CHUNKS:
-                transpose_ha(c + 1)
-            for j in range(HA_CHUNK):
-                t = c * HA_CHUNK + j
+        def adapter(r):
+            for a in range(ROUND):
+                t = r * ROUND + a
                 lora_ps = psum.tile([P, DIM], F32, tag="product")
-                nc.tensor.matmul(lora_ps[:], lhsT=haT_sb[c][:, j, :], rhs=b_sb[:], start=True, stop=True)
-                lora_sb = out_sb[t // ROUND][:, t % ROUND, :]
-                if t % 3 == 2:
-                    nc.vector.tensor_copy(out=lora_sb, in_=lora_ps[:])
-                else:
-                    nc.scalar.copy(out=lora_sb, in_=lora_ps[:])
-            if c < PASSES:
-                regroup_w2(c)
-            else:
-                quantise_w2(c - PASSES)
+                nc.tensor.matmul(
+                    lora_ps[:], lhsT=haT_sb[t // HA_CHUNK][:, t % HA_CHUNK, :], rhs=b_sb[:], start=True, stop=True
+                )
+                nc.scalar.copy(out=out_sb[r][:, a, :], in_=lora_ps[:])
+
+        w_grouped = keep.tile([P, PASSES, DIM, PACK], BF16, name="w_grouped", align_bytes=64)
+        w_codes = keep.tile([P, PASSES, DIM], U32, name="w_codes", align_bytes=64)
+        w_scales = keep.tile([P, PASSES, DIM], U8, name="w_scales", align_bytes=64)
+
+        def quantise_w2():
+            for g in range(PASSES):
+                nc.vector.tensor_copy(out=w_grouped[:, g], in_=w_raw[:, g].rearrange("q t n -> q n t"))
+            for g in range(PASSES):
+                nc.vector.quantize_mx(
+                    out=w_codes[:, g, :].bitcast(FP8X4),
+                    scales=w_scales[:, g, :],
+                    in_=w_grouped[:, g].rearrange("q n t -> q (n t)"),
+                )
 
         def transpose_h(r):
             h_words = h_sb[r][:].bitcast(F32)
-            grouped = []
+            h_grouped = stage.tile([P, ROUND, PASSES, P, PACK], BF16, tag="h_grouped", align_bytes=64)
             for a in range(ROUND):
                 hT_ps = psum.tile([P, PASSES * HALVES, P], F32, tag="transposed")
                 for s in range(PASSES * HALVES):
                     nc.tensor.transpose(hT_ps[:, s, :], h_words[:, a, s * P : (s + 1) * P], ident_f32[:])
-                h_grouped = stage.tile([P, PASSES, P, PACK], BF16, tag="h_grouped", align_bytes=64)
                 nc.scalar.copy(
-                    out=h_grouped[:].bitcast(F32),
+                    out=h_grouped[:, a].bitcast(F32),
                     in_=hT_ps[:].rearrange("q (g u) m -> q g m u", u=HALVES),
                 )
-                grouped.append(h_grouped)
-            return grouped
+            return h_grouped
 
         def quantise_h(h_grouped):
-            h_codes = stage.tile([P, PASSES, P], U32, tag="h_codes", align_bytes=64)
-            h_scales = stage.tile([P, PASSES, P], U8, tag="h_scales", align_bytes=64)
+            h_codes = stage.tile([P, ROUND, PASSES, P], U32, tag="h_codes", align_bytes=64)
+            h_scales = stage.tile([P, ROUND, PASSES, P], U8, tag="h_scales", align_bytes=64)
             nc.vector.quantize_mx(
-                out=h_codes[:].rearrange("q g m -> q (g m)").bitcast(FP8X4),
-                scales=h_scales[:].rearrange("q g m -> q (g m)"),
-                in_=h_grouped[:].rearrange("q g m t -> q (g m t)"),
+                out=h_codes[:].rearrange("q a g m -> q (a g m)").bitcast(FP8X4),
+                scales=h_scales[:].rearrange("q a g m -> q (a g m)"),
+                in_=h_grouped[:].rearrange("q a g m t -> q (a g m t)"),
             )
             return h_codes, h_scales
 
-        def project(r, a, h_codes, h_scales):
+        def project(h_codes, h_scales, a):
             base_ps = psum.tile([P, DIM], F32, tag="product")
             for g in range(PASSES):
                 nc.tensor.matmul_mx(
                     out=base_ps[:],
-                    lhsT=h_codes[:, g, :].bitcast(FP8X4),
-                    lhsT_scale=h_scales[:, g, :],
+                    lhsT=h_codes[:, a, g, :].bitcast(FP8X4),
+                    lhsT_scale=h_scales[:, a, g, :],
                     rhs=w_codes[:, g, :].bitcast(FP8X4),
                     rhs_scale=w_scales[:, g, :],
                     start=(g == 0),
@@ -155,16 +145,25 @@ def tile_feedforward_pb_t_kernel(tc, h, w2, ha_down, b_down, tw_down, out):
                 )
             return base_ps
 
-        quantised = [quantise_h(h_grouped) for h_grouped in transpose_h(0)]
+        transpose_ha(0)
+        for r in range(LEAD):
+            adapter(r)
+        quantise_w2()
+        for c in range(1, HA_CHUNKS):
+            transpose_ha(c)
+        ahead = quantise_h(transpose_h(0))
+
         for r in range(ROUNDS):
-            current = quantised
-            grouped = transpose_h(r + 1) if r + 1 < ROUNDS else []
-            quantised = []
+            h_codes, h_scales = ahead
+            if r + 1 < ROUNDS:
+                h_grouped = transpose_h(r + 1)
+            if r + LEAD < ROUNDS:
+                adapter(r + LEAD)
+            if r + 1 < ROUNDS:
+                ahead = quantise_h(h_grouped)
             for a in range(ROUND):
-                base_ps = project(r, a, current[a][0], current[a][1])
-                if grouped:
-                    quantised.append(quantise_h(grouped[a]))
                 t = r * ROUND + a
+                base_ps = project(h_codes, h_scales, a)
                 nc.vector.scalar_tensor_tensor(
                     out=out_sb[r][:, a, :],
                     in0=out_sb[r][:, a, :],
@@ -173,8 +172,4 @@ def tile_feedforward_pb_t_kernel(tc, h, w2, ha_down, b_down, tw_down, out):
                     op0=MULT,
                     op1=ADD,
                 )
-                if a % STORE == STORE - 1:
-                    first = r * ROUND + a + 1 - STORE
-                    nc.sync.dma_start(
-                        out=out_view[:, first : first + STORE, :], in_=out_sb[r][:, a + 1 - STORE : a + 1, :]
-                    )
+                nc.sync.dma_start(out=out_view[:, t, :], in_=out_sb[r][:, a, :])

@@ -56,7 +56,6 @@ def tile_feedforward_pb_t_kernel(tc, h, w2, ha_down, b_down, tw_down, out):
         def load_ha(c):
             nc.sync.dma_start(out=ha_sb[c][:], in_=ha_view[:, c * HA_CHUNK : (c + 1) * HA_CHUNK, :])
 
-        nc.sync.dma_start(out=tw_sb[:], in_=tw_view)
         load_ha(0)
         nc.sync.dma_start(out=b_sb[:], in_=b_down)
         for g in range(PASSES):
@@ -66,6 +65,7 @@ def tile_feedforward_pb_t_kernel(tc, h, w2, ha_down, b_down, tw_down, out):
             )
         for c in range(1, HA_CHUNKS):
             load_ha(c)
+        nc.sync.dma_start(out=tw_sb[:], in_=tw_view)
         for r in range(ROUNDS):
             nc.sync.dma_start(out=h_sb[r][:], in_=h_view[:, r * ROUND : (r + 1) * ROUND, :])
 
@@ -74,7 +74,6 @@ def tile_feedforward_pb_t_kernel(tc, h, w2, ha_down, b_down, tw_down, out):
         ident_f32 = keep.tile([P, P], F32, name="ident_f32")
         make_identity(nc, ident_f32[:])
         gain = keep.tile([P, TILES], F32, name="gain")
-        nc.vector.tensor_scalar_mul(out=gain[:], in0=tw_sb[:], scalar1=SCALING)
 
         haT_sb = [keep.tile([P, HA_CHUNK, P], BF16, name="haT%d" % c) for c in range(HA_CHUNKS)]
         out_sb = [keep.tile([P, ROUND, DIM], F32, name="out%d" % r) for r in range(ROUNDS)]
@@ -121,15 +120,17 @@ def tile_feedforward_pb_t_kernel(tc, h, w2, ha_down, b_down, tw_down, out):
                 )
             return h_grouped
 
-        def quantise_h(h_grouped):
+        def quantised_tiles():
             h_codes = stage.tile([P, ROUND, PASSES, P], U32, tag="h_codes", align_bytes=64)
             h_scales = stage.tile([P, ROUND, PASSES, P], U8, tag="h_scales", align_bytes=64)
-            nc.vector.quantize_mx(
-                out=h_codes[:].rearrange("q a g m -> q (a g m)").bitcast(FP8X4),
-                scales=h_scales[:].rearrange("q a g m -> q (a g m)"),
-                in_=h_grouped[:].rearrange("q a g m t -> q (a g m t)"),
-            )
             return h_codes, h_scales
+
+        def quantise_h(h_grouped, h_codes, h_scales, a):
+            nc.vector.quantize_mx(
+                out=h_codes[:, a].rearrange("q g m -> q (g m)").bitcast(FP8X4),
+                scales=h_scales[:, a].rearrange("q g m -> q (g m)"),
+                in_=h_grouped[:, a].rearrange("q g m t -> q (g m t)"),
+            )
 
         def project(h_codes, h_scales, a):
             base_ps = psum.tile([P, DIM], F32, tag="product")
@@ -151,19 +152,24 @@ def tile_feedforward_pb_t_kernel(tc, h, w2, ha_down, b_down, tw_down, out):
         quantise_w2()
         for c in range(1, HA_CHUNKS):
             transpose_ha(c)
-        ahead = quantise_h(transpose_h(0))
+        nc.vector.tensor_scalar_mul(out=gain[:], in0=tw_sb[:], scalar1=SCALING)
+        h_grouped = transpose_h(0)
+        ahead = quantised_tiles()
+        for a in range(ROUND):
+            quantise_h(h_grouped, ahead[0], ahead[1], a)
 
         for r in range(ROUNDS):
             h_codes, h_scales = ahead
             if r + 1 < ROUNDS:
                 h_grouped = transpose_h(r + 1)
+                ahead = quantised_tiles()
             if r + LEAD < ROUNDS:
                 adapter(r + LEAD)
-            if r + 1 < ROUNDS:
-                ahead = quantise_h(h_grouped)
             for a in range(ROUND):
                 t = r * ROUND + a
                 base_ps = project(h_codes, h_scales, a)
+                if r + 1 < ROUNDS:
+                    quantise_h(h_grouped, ahead[0], ahead[1], a)
                 nc.vector.scalar_tensor_tensor(
                     out=out_sb[r][:, a, :],
                     in0=out_sb[r][:, a, :],

@@ -84,8 +84,8 @@ def tile_feedforward_pb_t_kernel(tc, h, w2, ha_down, b_down, tw_down, out):
                 nc.tensor.transpose(haT_ps[:, j, :], ha_sb[c][:, j, :], ident_bf16[:])
             nc.vector.tensor_copy(out=haT_sb[c][:], in_=haT_ps[:])
 
-        def adapter(r):
-            for a in range(ROUND):
+        def adapter(r, tiles_of_round):
+            for a in tiles_of_round:
                 t = r * ROUND + a
                 lora_ps = psum.tile([P, DIM], F32, tag="product")
                 nc.tensor.matmul(
@@ -148,7 +148,7 @@ def tile_feedforward_pb_t_kernel(tc, h, w2, ha_down, b_down, tw_down, out):
 
         transpose_ha(0)
         for r in range(LEAD):
-            adapter(r)
+            adapter(r, range(ROUND))
         quantise_w2()
         for c in range(1, HA_CHUNKS):
             transpose_ha(c)
@@ -164,7 +164,7 @@ def tile_feedforward_pb_t_kernel(tc, h, w2, ha_down, b_down, tw_down, out):
                 h_grouped = transpose_h(r + 1)
                 ahead = quantised_tiles()
             if r + LEAD < ROUNDS:
-                adapter(r + LEAD)
+                adapter(r + LEAD, range(0, ROUND // 2))
             for a in range(ROUND):
                 t = r * ROUND + a
                 base_ps = project(h_codes, h_scales, a)
@@ -179,3 +179,5 @@ def tile_feedforward_pb_t_kernel(tc, h, w2, ha_down, b_down, tw_down, out):
                     op1=ADD,
                 )
                 nc.sync.dma_start(out=out_view[:, t, :], in_=out_sb[r][:, a, :])
+            if r + LEAD < ROUNDS:
+                adapter(r + LEAD, range(ROUND // 2, ROUND))

@@ -56,6 +56,7 @@ def tile_feedforward_pb_t_kernel(tc, h, w2, ha_down, b_down, tw_down, out):
         def load_ha(c):
             nc.sync.dma_start(out=ha_sb[c][:], in_=ha_view[:, c * HA_CHUNK : (c + 1) * HA_CHUNK, :])
 
+        nc.sync.dma_start(out=tw_sb[:], in_=tw_view)
         load_ha(0)
         nc.sync.dma_start(out=b_sb[:], in_=b_down)
         for g in range(PASSES):
@@ -65,7 +66,6 @@ def tile_feedforward_pb_t_kernel(tc, h, w2, ha_down, b_down, tw_down, out):
             )
         for c in range(1, HA_CHUNKS):
             load_ha(c)
-        nc.sync.dma_start(out=tw_sb[:], in_=tw_view)
         for r in range(ROUNDS):
             nc.sync.dma_start(out=h_sb[r][:], in_=h_view[:, r * ROUND : (r + 1) * ROUND, :])
 

from contextlib import ExitStack

import concourse.mybir as mybir
from concourse.masks import make_identity

BF16 = mybir.dt.bfloat16
F32 = mybir.dt.float32
U32 = mybir.dt.uint32
U8 = mybir.dt.uint8
FP8X4 = mybir.dt.float8_e4m3fn_x4
MULT = mybir.AluOpType.mult
ADD = mybir.AluOpType.add

P = 128
TOKENS = 8 * 512
HID = 1024
DIM = 512
RANK = 128
SCALING = 4.0

PACK = 4
K_PASS = P * PACK
PASSES = HID // K_PASS
HALVES = 2

TILES = TOKENS // P
ROUND = 2
ROUNDS = TILES // ROUND
HA_CHUNK = 8
HA_CHUNKS = TILES // HA_CHUNK
LEAD = HA_CHUNK // ROUND
BANKS = 4

FLOPS = 2 * TOKENS * HID * DIM + 2 * TOKENS * RANK * DIM


def tile_feedforward_pb_t_kernel(tc, h, w2, ha_down, b_down, tw_down, out):
    nc = tc.nc
    h_view = h.flatten_outer_dims().rearrange("(p t) k -> p t k", t=TILES)
    ha_view = ha_down.flatten_outer_dims().rearrange("(p t) r -> p t r", t=TILES)
    tw_view = tw_down.rearrange("b (q t) -> (b q) t", t=TILES)
    out_view = out.flatten_outer_dims().rearrange("(p t) n -> p t n", t=TILES)

    with ExitStack() as ctx:
        keep = ctx.enter_context(tc.tile_pool(name="keep", bufs=1))
        stage = ctx.enter_context(tc.tile_pool(name="stage", bufs=3))
        psum = ctx.enter_context(tc.psum_pool(name="psum", bufs=BANKS))
        ctx.enter_context(tc.manual_schedule())

        tw_sb = keep.tile([P, TILES], BF16, name="tw_sb")
        ha_sb = [keep.tile([P, HA_CHUNK, RANK], BF16, name="ha%d" % c) for c in range(HA_CHUNKS)]
        b_sb = keep.tile([P, DIM], BF16, name="b_sb")
        w_raw = keep.tile([P, PASSES, PACK, DIM], BF16, name="w_raw")
        h_sb = [keep.tile([P, ROUND, HID], BF16, name="h%d" % r) for r in range(ROUNDS)]

        def load_ha(c):
            nc.sync.dma_start(out=ha_sb[c][:], in_=ha_view[:, c * HA_CHUNK : (c + 1) * HA_CHUNK, :])

        nc.sync.dma_start(out=tw_sb[:], in_=tw_view)
        load_ha(0)
        nc.sync.dma_start(out=b_sb[:], in_=b_down)
        for g in range(PASSES):
            nc.sync.dma_start(
                out=w_raw[:, g].rearrange("q (u e) n -> q u e n", u=HALVES),
                in_=w2[g * K_PASS : (g + 1) * K_PASS, :].rearrange("(u q e) n -> q u e n", u=HALVES, q=P),
            )
        for c in range(1, HA_CHUNKS):
            load_ha(c)
        for r in range(ROUNDS):
            nc.sync.dma_start(out=h_sb[r][:], in_=h_view[:, r * ROUND : (r + 1) * ROUND, :])

        ident_bf16 = keep.tile([P, P], BF16, name="ident_bf16")
        make_identity(nc, ident_bf16[:])
        ident_f32 = keep.tile([P, P], F32, name="ident_f32")
        make_identity(nc, ident_f32[:])
        gain = keep.tile([P, TILES], F32, name="gain")

        haT_sb = [keep.tile([P, HA_CHUNK, P], BF16, name="haT%d" % c) for c in range(HA_CHUNKS)]
        out_sb = [keep.tile([P, ROUND, DIM], F32, name="out%d" % r) for r in range(ROUNDS)]

        def transpose_ha(c):
            haT_ps = psum.tile([P, HA_CHUNK, P], BF16, tag="transposed")
            for j in range(HA_CHUNK):
                nc.tensor.transpose(haT_ps[:, j, :], ha_sb[c][:, j, :], ident_bf16[:])
            nc.vector.tensor_copy(out=haT_sb[c][:], in_=haT_ps[:])

        def adapter(r, tiles_of_round):
            for a in tiles_of_round:
                t = r * ROUND + a
                lora_ps = psum.tile([P, DIM], F32, tag="product")
                nc.tensor.matmul(
                    lora_ps[:], lhsT=haT_sb[t // HA_CHUNK][:, t % HA_CHUNK, :], rhs=b_sb[:], start=True, stop=True
                )
                nc.scalar.copy(out=out_sb[r][:, a, :], in_=lora_ps[:])

        w_grouped = keep.tile([P, PASSES, DIM, PACK], BF16, name="w_grouped", align_bytes=64)
        w_codes = keep.tile([P, PASSES, DIM], U32, name="w_codes", align_bytes=64)
        w_scales = keep.tile([P, PASSES, DIM], U8, name="w_scales", align_bytes=64)

        def quantise_w2():
            for g in range(PASSES):
                nc.vector.tensor_copy(out=w_grouped[:, g], in_=w_raw[:, g].rearrange("q t n -> q n t"))
            for g in range(PASSES):
                nc.vector.quantize_mx(
                    out=w_codes[:, g, :].bitcast(FP8X4),
                    scales=w_scales[:, g, :],
                    in_=w_grouped[:, g].rearrange("q n t -> q (n t)"),
                )

        def transpose_h(r):
            h_words = h_sb[r][:].bitcast(F32)
            h_grouped = stage.tile([P, ROUND, PASSES, P, PACK], BF16, tag="h_grouped", align_bytes=64)
            for a in range(ROUND):
                hT_ps = psum.tile([P, PASSES * HALVES, P], F32, tag="transposed")
                for s in range(PASSES * HALVES):
                    nc.tensor.transpose(hT_ps[:, s, :], h_words[:, a, s * P : (s + 1) * P], ident_f32[:])
                nc.scalar.copy(
                    out=h_grouped[:, a].bitcast(F32),
                    in_=hT_ps[:].rearrange("q (g u) m -> q g m u", u=HALVES),
                )
            return h_grouped

        def quantised_tiles():
            h_codes = stage.tile([P, ROUND, PASSES, P], U32, tag="h_codes", align_bytes=64)
            h_scales = stage.tile([P, ROUND, PASSES, P], U8, tag="h_scales", align_bytes=64)
            return h_codes, h_scales

        def quantise_h(h_grouped, h_codes, h_scales, a):
            nc.vector.quantize_mx(
                out=h_codes[:, a].rearrange("q g m -> q (g m)").bitcast(FP8X4),
                scales=h_scales[:, a].rearrange("q g m -> q (g m)"),
                in_=h_grouped[:, a].rearrange("q g m t -> q (g m t)"),
            )

        def project(h_codes, h_scales, a):
            base_ps = psum.tile([P, DIM], F32, tag="product")
            for g in range(PASSES):
                nc.tensor.matmul_mx(
                    out=base_ps[:],
                    lhsT=h_codes[:, a, g, :].bitcast(FP8X4),
                    lhsT_scale=h_scales[:, a, g, :],
                    rhs=w_codes[:, g, :].bitcast(FP8X4),
                    rhs_scale=w_scales[:, g, :],
                    start=(g == 0),
                    stop=(g == PASSES - 1),
                )
            return base_ps

        transpose_ha(0)
        for r in range(LEAD):
            adapter(r, range(ROUND))
        quantise_w2()
        for c in range(1, HA_CHUNKS):
            transpose_ha(c)
        nc.vector.tensor_scalar_mul(out=gain[:], in0=tw_sb[:], scalar1=SCALING)
        h_grouped = transpose_h(0)
        ahead = quantised_tiles()
        for a in range(ROUND):
            quantise_h(h_grouped, ahead[0], ahead[1], a)

        for r in range(ROUNDS):
            h_codes, h_scales = ahead
            if r + 1 < ROUNDS:
                h_grouped = transpose_h(r + 1)
                ahead = quantised_tiles()
            if r + LEAD < ROUNDS:
                adapter(r + LEAD, range(0, ROUND // 2))
            for a in range(ROUND):
                t = r * ROUND + a
                base_ps = project(h_codes, h_scales, a)
                if r + 1 < ROUNDS:
                    quantise_h(h_grouped, ahead[0], ahead[1], a)
                nc.vector.scalar_tensor_tensor(
                    out=out_sb[r][:, a, :],
                    in0=out_sb[r][:, a, :],
                    scalar=gain[:, t : t + 1],
                    in1=base_ps[:],
                    op0=MULT,
                    op1=ADD,
                )
                nc.sync.dma_start(out=out_view[:, t, :], in_=out_sb[r][:, a, :])
            if r + LEAD < ROUNDS:
                adapter(r + LEAD, range(ROUND // 2, ROUND))
